import numpy as np
import ml_dtypes


def mxq(x, axis, fmt="e4m3"):
    dtype, down = {"e4m3": (ml_dtypes.float8_e4m3fn, 7), "e5m2": (ml_dtypes.float8_e5m2, 14)}[fmt]
    v = np.moveaxis(np.asarray(x, np.float32).astype(ml_dtypes.bfloat16).astype(np.float64), axis, -1)
    blocks = v.reshape(v.shape[:-1] + (-1, 32))
    amax = np.abs(blocks).max(-1, keepdims=True)
    byte = np.maximum(np.where(amax > 0, np.frexp(amax)[1] - 1 + 127, 0) - down, 1)
    scale = np.exp2(byte - 127.0)
    codes = (blocks / scale).astype(np.float32).astype(dtype).astype(np.float64)
    return np.moveaxis((codes * scale).reshape(v.shape), -1, axis)


WIDE = False


def mx_kscale(k):
    if not WIDE:
        return np.ones(k)
    levels = np.array([10, -10, 5, -5, 0])
    a = np.random.permutation(np.resize(levels, k // 512 * 4)).reshape(k // 512, 4)
    idx = np.arange(k)
    return np.exp2(a[idx // 512, idx % 128 // 32])


BF16 = ml_dtypes.bfloat16


def bf(x):
    return np.asarray(x, np.float32).astype(BF16)


def f64(x):
    return np.asarray(x).astype(np.float64)


N, D, C, M = 256, 16384, 16, 16
LAMDA = 0.00390625
VS = 1.0 / (LAMDA * D)


def setup_inputs():
    s = mx_kscale(D)
    return {"x": bf(np.random.standard_normal((N, D)) * s),
            "x_var": bf(np.random.uniform(0.0, 1.0, (N, D)) * (0.5 + np.random.uniform(0.0, 1.0, (N, 1))) * 2.0 * VS),
            "proto_mean": bf(np.random.standard_normal((C, M, D)) / np.sqrt(D) / s),
            "proto_var": bf(np.random.uniform(0.0, 1.0, (C, M, D)) * (0.5 + np.random.uniform(0.0, 1.0, (C, M, 1))) * 2.0 * VS)}


def reference(x, x_var, proto_mean, proto_var):
    xv, pv = f64(x_var), f64(proto_var)
    dot = (mxq(f64(x), 1, "e4m3") @ mxq(f64(proto_mean), 2, "e4m3").reshape(C * M, D).T).reshape(N, C, M)
    cross = (mxq(np.sqrt(xv), 1, "e4m3") @ mxq(np.sqrt(pv), 2, "e4m3").reshape(C * M, D).T).reshape(N, C, M)
    var_term = xv.sum(-1)[:, None, None] + pv.sum(-1)[None, :, :] - 2.0 * cross
    return -(2.0 - 2.0 * dot + LAMDA * var_term)

@@ -1,0 +1,239 @@
+from contextlib import ExitStack
+
+import concourse.mybir as mybir
+from concourse.masks import make_identity
+
+F32 = mybir.dt.float32
+BF16 = mybir.dt.bfloat16
+U32 = mybir.dt.uint32
+U8 = mybir.dt.uint8
+FP8X4 = mybir.dt.float8_e4m3fn_x4
+ACT = mybir.ActivationFunctionType
+ALU = mybir.AluOpType
+AXIS = mybir.AxisListType
+
+LAMDA = 0.00390625
+
+P = 128
+ROWS = 256
+ROW_TILES = ROWS // P
+D = 16384
+K_PASS = 4 * P
+PASSES = D // K_PASS
+PASS_WORDS = K_PASS // 2
+CHUNK = 1024
+CHUNK_WORDS = CHUNK // 2
+CHUNK_PASSES = CHUNK // K_PASS
+CHUNKS = D // CHUNK
+CHUNK_BUFS = 8
+GROUPED = ROWS * 4
+
+FLOPS = 2 * 2 * ROWS * ROWS * D
+
+VARIANCES = ("xv", "pv")
+INPUTS = ("xv", "pv", "x", "pm")
+
+
+def tile_probprotoseghead_k_kernel(tc, x, x_var, proto_mean, proto_var, out):
+    nc = tc.nc
+    with ExitStack() as ctx:
+        ctx.enter_context(tc.manual_schedule())
+        const = ctx.enter_context(tc.tile_pool(name="const", bufs=1))
+        chunks = ctx.enter_context(tc.tile_pool(name="chunks", bufs=CHUNK_BUFS))
+        stage = ctx.enter_context(tc.tile_pool(name="stage", bufs=3))
+        banks = ctx.enter_context(tc.psum_pool(name="banks", bufs=1))
+        sums = ctx.enter_context(tc.psum_pool(name="sums", bufs=1))
+
+        dram = {
+            "x": x.rearrange("(t p) d -> p t d", p=P),
+            "xv": x_var.rearrange("(t p) d -> p t d", p=P),
+            "pm": proto_mean.rearrange("c m d -> (c m) d").rearrange("(t p) d -> p t d", p=P),
+            "pv": proto_var.rearrange("c m d -> (c m) d").rearrange("(t p) d -> p t d", p=P),
+        }
+        out_rows = out.rearrange("(t p) c m -> p t (c m)", p=P)
+
+        identity = const.tile([P, P], F32, name="identity")
+        make_identity(nc, identity[:])
+
+        one = const.tile([P, 1], F32, name="one")
+        nc.vector.memset(one[:], 1.0)
+        warm = const.tile([P, 1], F32, name="warm")
+        nc.scalar.activation(out=warm[:], in_=one[:], func=ACT.Sqrt)
+
+        dot = [sums.tile([P, ROWS], F32, name="dot%d" % t) for t in range(ROW_TILES)]
+        cross = [sums.tile([P, ROWS], F32, name="cross%d" % t) for t in range(ROW_TILES)]
+
+        pieces = const.tile([P, 2 * ROW_TILES * CHUNKS], F32, name="pieces")
+
+        resident = {}
+        in_psum = {}
+        grouped = {}
+        packed = {}
+
+        def load(c):
+            for name in INPUTS:
+                rows = chunks.tile([P, ROW_TILES * CHUNK], BF16, name="rows_" + name, tag=name)
+                nc.sync.dma_start(
+                    out=rows[:].rearrange("p (t d) -> p t d", t=ROW_TILES),
+                    in_=dram[name][:, :, c * CHUNK : (c + 1) * CHUNK],
+                )
+                resident[(name, c)] = rows
+
+        def add_rows(g):
+            c, i = divmod(g, CHUNK_PASSES)
+            rows = resident[(VARIANCES[i], c)]
+            for t in range(ROW_TILES):
+                j = i * ROW_TILES + t
+                pair_sums = stage.tile([P, CHUNK // 2], F32, name="pair_sums")
+                nc.vector.scalar_tensor_tensor(
+                    out=pair_sums[:],
+                    in0=rows[:, t * CHUNK : t * CHUNK + CHUNK // 2],
+                    scalar=1.0,
+                    in1=rows[:, t * CHUNK + CHUNK // 2 : (t + 1) * CHUNK],
+                    op0=ALU.mult,
+                    op1=ALU.add,
+                    accum_out=pieces[:, j * CHUNKS + c : j * CHUNKS + c + 1],
+                )
+
+        def transposes(g):
+            c, local = divmod(g, CHUNK_PASSES)
+            for name in INPUTS:
+                words = resident[(name, c)][:].bitcast(F32)
+                bank = banks.tile([P, 2 * ROWS], F32, name="bank_" + name, tag=name)
+                for u in range(2):
+                    for t in range(ROW_TILES):
+                        first = t * CHUNK_WORDS + local * PASS_WORDS + u * P
+                        nc.tensor.transpose(
+                            bank[:, u * ROWS + t * P : u * ROWS + (t + 1) * P],
+                            words[:, first : first + P],
+                            identity[:],
+                        )
+                in_psum[name] = bank
+
+        def leave_psum():
+            mean = stage.tile([P, 2 * GROUPED], BF16, name="mean", align_bytes=64)
+            var = stage.tile([P, 2 * GROUPED], BF16, name="var", align_bytes=64)
+            for i, name in enumerate(VARIANCES):
+                nc.scalar.activation(
+                    out=var[:, i * GROUPED : (i + 1) * GROUPED].rearrange(
+                        "p (r u e) -> p r u e", u=2, e=2
+                    ),
+                    in_=in_psum[name][:].bitcast(BF16).rearrange("p (u r e) -> p r u e", u=2, e=2),
+                    func=ACT.Sqrt,
+                )
+            mean_words = mean[:].bitcast(F32)
+            nc.scalar.copy(
+                out=mean_words[:, 0 : 2 * ROWS].rearrange("p (r u) -> p r u", u=2),
+                in_=in_psum["x"][:].rearrange("p (u r) -> p r u", u=2),
+            )
+            nc.vector.tensor_copy(
+                out=mean_words[:, 2 * ROWS : 4 * ROWS].rearrange("p (r u) -> p r u", u=2),
+                in_=in_psum["pm"][:].rearrange("p (u r) -> p r u", u=2),
+            )
+            grouped["mean"] = mean
+            grouped["var"] = var
+
+        def quantise():
+            for kind in ("var", "mean"):
+                words = stage.tile([P, 2 * ROWS], U32, name="words_" + kind, align_bytes=64)
+                scales = stage.tile([P, 2 * ROWS], U8, name="scales_" + kind, align_bytes=64)
+                nc.vector.quantize_mx(
+                    out=words[:].bitcast(FP8X4), scales=scales[:], in_=grouped[kind][:]
+                )
+                packed[kind] = (words, scales)
+
+        def multiply(g):
+            for kind, acc in (("var", cross), ("mean", dot)):
+                words, scales = packed[kind]
+                for t in range(ROW_TILES):
+                    nc.tensor.matmul_mx(
+                        out=acc[t][:],
+                        lhsT=words[:, t * P : (t + 1) * P].bitcast(FP8X4),
+                        lhsT_scale=scales[:, t * P : (t + 1) * P],
+                        rhs=words[:, ROWS : 2 * ROWS].bitcast(FP8X4),
+                        rhs_scale=scales[:, ROWS : 2 * ROWS],
+                        start=(g == 0),
+                        stop=(g == PASSES - 1),
+                    )
+
+        totals = const.tile([P, 2 * ROW_TILES], F32, name="totals")
+        row_term = const.tile([P, ROW_TILES], F32, name="row_term")
+        repeated = const.tile([P, ROWS], F32, name="repeated")
+
+        def total_rows():
+            nc.vector.tensor_reduce(
+                out=totals[:],
+                in_=pieces[:].rearrange("p (j c) -> p j c", c=CHUNKS),
+                axis=AXIS.X,
+                op=ALU.add,
+            )
+            nc.vector.tensor_scalar(
+                out=row_term[:],
+                in0=totals[:, 0:ROW_TILES],
+                scalar1=-LAMDA,
+                scalar2=-2.0,
+                op0=ALU.mult,
+                op1=ALU.add,
+            )
+            for t in range(ROW_TILES):
+                nc.vector.tensor_scalar(
+                    out=repeated[:, t * P : (t + 1) * P],
+                    in0=totals[:, ROW_TILES + t : ROW_TILES + t + 1].to_broadcast([P, P]),
+                    scalar1=-LAMDA,
+                    scalar2=None,
+                    op0=ALU.mult,
+                )
+
+        for c in range(CHUNK_BUFS):
+            load(c)
+
+        for g in range(PASSES):
+            transposes(g)
+            if g >= 1:
+                quantise()
+            add_rows(g)
+            leave_psum()
+            if g >= 1:
+                multiply(g - 1)
+            if (g + 1) % CHUNK_PASSES == 0 and g // CHUNK_PASSES + CHUNK_BUFS < CHUNKS:
+                load(g // CHUNK_PASSES + CHUNK_BUFS)
+        total_rows()
+
+        spread = banks.tile([P, ROWS], F32, name="spread", tag="xv")
+        for t in range(ROW_TILES):
+            nc.tensor.transpose(
+                spread[:, t * P : (t + 1) * P], repeated[:, t * P : (t + 1) * P], identity[:]
+            )
+        quantise()
+        multiply(PASSES - 1)
+
+        plain = const.tile([P, ROW_TILES * ROWS], F32, name="plain")
+        for t in range(ROW_TILES):
+            nc.vector.tensor_scalar(
+                out=plain[:, t * ROWS : (t + 1) * ROWS],
+                in0=spread[:],
+                scalar1=row_term[:, t : t + 1],
+                scalar2=None,
+                op0=ALU.add,
+            )
+        with_cross = const.tile([P, ROW_TILES * ROWS], F32, name="with_cross")
+        result = const.tile([P, ROW_TILES * ROWS], F32, name="result")
+        for t in range(ROW_TILES):
+            nc.vector.scalar_tensor_tensor(
+                out=with_cross[:, t * ROWS : (t + 1) * ROWS],
+                in0=cross[t][:],
+                scalar=2.0 * LAMDA,
+                in1=plain[:, t * ROWS : (t + 1) * ROWS],
+                op0=ALU.mult,
+                op1=ALU.add,
+            )
+        for t in range(ROW_TILES):
+            nc.vector.scalar_tensor_tensor(
+                out=result[:, t * ROWS : (t + 1) * ROWS],
+                in0=dot[t][:],
+                scalar=2.0,
+                in1=with_cross[:, t * ROWS : (t + 1) * ROWS],
+                op0=ALU.mult,
+                op1=ALU.add,
+            )
+            nc.sync.dma_start(out=out_rows[:, t, :], in_=result[:, t * ROWS : (t + 1) * ROWS])

@@ -25,12 +25,18 @@ CHUNK = 1024
 CHUNK_WORDS = CHUNK // 2
 CHUNK_PASSES = CHUNK // K_PASS
 CHUNKS = D // CHUNK
+CHUNK_PAIRS = CHUNKS // 2
+SUM_LAG = 5
+TENSOR_PAIRS = 6
+FOLDED_PASSES = TENSOR_PAIRS * 2 * CHUNK_PASSES
 CHUNK_BUFS = 8
 GROUPED = ROWS * 4
 
 FLOPS = 2 * 2 * ROWS * ROWS * D
 
 VARIANCES = ("xv", "pv")
+MEANS = ("x", "pm")
+VAR_BANKS = 3
 INPUTS = ("xv", "pv", "x", "pm")
 
 
@@ -54,16 +60,25 @@ def tile_probprotoseghead_k_kernel(tc, x, x_var, proto_mean, proto_var, out):
 
         identity = const.tile([P, P], F32, name="identity")
         make_identity(nc, identity[:])
+        identity_bf16 = const.tile([P, P], BF16, name="identity_bf16")
+        make_identity(nc, identity_bf16[:])
 
         one = const.tile([P, 1], F32, name="one")
         nc.vector.memset(one[:], 1.0)
         warm = const.tile([P, 1], F32, name="warm")
         nc.scalar.activation(out=warm[:], in_=one[:], func=ACT.Sqrt)
 
-        dot = [sums.tile([P, ROWS], F32, name="dot%d" % t) for t in range(ROW_TILES)]
-        cross = [sums.tile([P, ROWS], F32, name="cross%d" % t) for t in range(ROW_TILES)]
+        product = [sums.tile([P, ROWS], F32, name="product%d" % t) for t in range(ROW_TILES)]
 
-        pieces = const.tile([P, 2 * ROW_TILES * CHUNKS], F32, name="pieces")
+        pieces = const.tile([P, 2 * ROW_TILES * CHUNK_PAIRS], F32, name="pieces")
+        nc.vector.memset(pieces[:], 0.0)
+        folded = sums.tile([P, K_PASS], F32, name="folded")
+        vector_sums = [
+            (j, i)
+            for j in range(CHUNK_PAIRS)
+            for i in range(2 * ROW_TILES)
+            if i > 0 or j >= TENSOR_PAIRS
+        ]
 
         resident = {}
         in_psum = {}
@@ -79,27 +94,46 @@ def tile_probprotoseghead_k_kernel(tc, x, x_var, proto_mean, proto_var, out):
                 )
                 resident[(name, c)] = rows
 
-        def add_rows(g):
-            c, i = divmod(g, CHUNK_PASSES)
-            rows = resident[(VARIANCES[i], c)]
-            for t in range(ROW_TILES):
-                j = i * ROW_TILES + t
-                pair_sums = stage.tile([P, CHUNK // 2], F32, name="pair_sums")
-                nc.vector.scalar_tensor_tensor(
-                    out=pair_sums[:],
-                    in0=rows[:, t * CHUNK : t * CHUNK + CHUNK // 2],
-                    scalar=1.0,
-                    in1=rows[:, t * CHUNK + CHUNK // 2 : (t + 1) * CHUNK],
-                    op0=ALU.mult,
-                    op1=ALU.add,
-                    accum_out=pieces[:, j * CHUNKS + c : j * CHUNKS + c + 1],
-                )
+        def add_rows(k):
+            j, i = vector_sums[k]
+            name, t = VARIANCES[i // ROW_TILES], i % ROW_TILES
+            halves = [
+                resident[(name, c)][:, t * CHUNK : (t + 1) * CHUNK] for c in (2 * j, 2 * j + 1)
+            ]
+            pair_sums = stage.tile([P, CHUNK], F32, name="pair_sums")
+            nc.vector.scalar_tensor_tensor(
+                out=pair_sums[:],
+                in0=halves[0],
+                scalar=1.0,
+                in1=halves[1],
+                op0=ALU.mult,
+                op1=ALU.add,
+                accum_out=pieces[:, i * CHUNK_PAIRS + j : i * CHUNK_PAIRS + j + 1],
+            )
 
-        def transposes(g):
+        def fold_rows(g):
             c, local = divmod(g, CHUNK_PASSES)
-            for name in INPUTS:
+            nc.tensor.matmul(
+                folded[:],
+                lhsT=identity_bf16[:],
+                rhs=resident[("xv", c)][:, local * K_PASS : (local + 1) * K_PASS],
+                start=(g == 0),
+                stop=(g == FOLDED_PASSES - 1),
+            )
+
+        def add_folded():
+            nc.vector.tensor_reduce(
+                out=pieces[:, 0:1], in_=folded[:], axis=AXIS.X, op=ALU.add
+            )
+
+        def transposes(g, names):
+            c, local = divmod(g, CHUNK_PASSES)
+            for name in names:
                 words = resident[(name, c)][:].bitcast(F32)
-                bank = banks.tile([P, 2 * ROWS], F32, name="bank_" + name, tag=name)
+                if name in VARIANCES:
+                    bank = banks.tile([P, 2 * ROWS], F32, name="bank_var", tag="var", bufs=VAR_BANKS)
+                else:
+                    bank = banks.tile([P, 2 * ROWS], F32, name="bank_" + name, tag=name)
                 for u in range(2):
                     for t in range(ROW_TILES):
                         first = t * CHUNK_WORDS + local * PASS_WORDS + u * P
@@ -108,9 +142,9 @@ def tile_probprotoseghead_k_kernel(tc, x, x_var, proto_mean, proto_var, out):
                             words[:, first : first + P],
                             identity[:],
                         )
-                in_psum[name] = bank
+                in_psum[(name, g)] = bank
 
-        def leave_psum():
+        def leave_psum(g):
             mean = stage.tile([P, 2 * GROUPED], BF16, name="mean", align_bytes=64)
             var = stage.tile([P, 2 * GROUPED], BF16, name="var", align_bytes=64)
             for i, name in enumerate(VARIANCES):
@@ -118,17 +152,18 @@ def tile_probprotoseghead_k_kernel(tc, x, x_var, proto_mean, proto_var, out):
                     out=var[:, i * GROUPED : (i + 1) * GROUPED].rearrange(
                         "p (r u e) -> p r u e", u=2, e=2
                     ),
-                    in_=in_psum[name][:].bitcast(BF16).rearrange("p (u r e) -> p r u e", u=2, e=2),
+                    in_=in_psum[(name, g)][:].bitcast(BF16).rearrange("p (u r e) -> p r u e", u=2, e=2),
                     func=ACT.Sqrt,
+                    scale=LAMDA,
                 )
             mean_words = mean[:].bitcast(F32)
             nc.scalar.copy(
                 out=mean_words[:, 0 : 2 * ROWS].rearrange("p (r u) -> p r u", u=2),
-                in_=in_psum["x"][:].rearrange("p (u r) -> p r u", u=2),
+                in_=in_psum[("x", g)][:].rearrange("p (u r) -> p r u", u=2),
             )
             nc.vector.tensor_copy(
                 out=mean_words[:, 2 * ROWS : 4 * ROWS].rearrange("p (r u) -> p r u", u=2),
-                in_=in_psum["pm"][:].rearrange("p (u r) -> p r u", u=2),
+                in_=in_psum[("pm", g)][:].rearrange("p (u r) -> p r u", u=2),
             )
             grouped["mean"] = mean
             grouped["var"] = var
@@ -143,17 +178,17 @@ def tile_probprotoseghead_k_kernel(tc, x, x_var, proto_mean, proto_var, out):
                 packed[kind] = (words, scales)
 
         def multiply(g):
-            for kind, acc in (("var", cross), ("mean", dot)):
+            for kind in ("var", "mean"):
                 words, scales = packed[kind]
                 for t in range(ROW_TILES):
                     nc.tensor.matmul_mx(
-                        out=acc[t][:],
+                        out=product[t][:],
                         lhsT=words[:, t * P : (t + 1) * P].bitcast(FP8X4),
                         lhsT_scale=scales[:, t * P : (t + 1) * P],
                         rhs=words[:, ROWS : 2 * ROWS].bitcast(FP8X4),
                         rhs_scale=scales[:, ROWS : 2 * ROWS],
-                        start=(g == 0),
-                        stop=(g == PASSES - 1),
+                        start=(g == 0 and kind == "var"),
+                        stop=(g == PASSES - 1 and kind == "mean"),
                     )
 
         totals = const.tile([P, 2 * ROW_TILES], F32, name="totals")
@@ -163,7 +198,7 @@ def tile_probprotoseghead_k_kernel(tc, x, x_var, proto_mean, proto_var, out):
         def total_rows():
             nc.vector.tensor_reduce(
                 out=totals[:],
-                in_=pieces[:].rearrange("p (j c) -> p j c", c=CHUNKS),
+                in_=pieces[:].rearrange("p (i j) -> p i j", j=CHUNK_PAIRS),
                 axis=AXIS.X,
                 op=ALU.add,
             )
@@ -187,19 +222,30 @@ def tile_probprotoseghead_k_kernel(tc, x, x_var, proto_mean, proto_var, out):
         for c in range(CHUNK_BUFS):
             load(c)
 
+        transposes(0, VARIANCES)
         for g in range(PASSES):
-            transposes(g)
+            transposes(g, MEANS)
+            if g + 1 < PASSES:
+                transposes(g + 1, VARIANCES)
             if g >= 1:
                 quantise()
-            add_rows(g)
-            leave_psum()
+            if 0 <= g - SUM_LAG < len(vector_sums):
+                add_rows(g - SUM_LAG)
+            if g == PASSES - SUM_LAG:
+                add_folded()
+            leave_psum(g)
             if g >= 1:
                 multiply(g - 1)
-            if (g + 1) % CHUNK_PASSES == 0 and g // CHUNK_PASSES + CHUNK_BUFS < CHUNKS:
-                load(g // CHUNK_PASSES + CHUNK_BUFS)
+            if g < FOLDED_PASSES:
+                fold_rows(g)
+            if 0 <= g - SUM_LAG < len(vector_sums):
+                j, i = vector_sums[g - SUM_LAG]
+                if i == 2 * ROW_TILES - 1 and 2 * j + CHUNK_BUFS < CHUNKS:
+                    load(2 * j + CHUNK_BUFS)
+                    load(2 * j + 1 + CHUNK_BUFS)
         total_rows()
 
-        spread = banks.tile([P, ROWS], F32, name="spread", tag="xv")
+        spread = banks.tile([P, ROWS], F32, name="spread", tag="x")
         for t in range(ROW_TILES):
             nc.tensor.transpose(
                 spread[:, t * P : (t + 1) * P], repeated[:, t * P : (t + 1) * P], identity[:]
@@ -216,23 +262,13 @@ def tile_probprotoseghead_k_kernel(tc, x, x_var, proto_mean, proto_var, out):
                 scalar2=None,
                 op0=ALU.add,
             )
-        with_cross = const.tile([P, ROW_TILES * ROWS], F32, name="with_cross")
         result = const.tile([P, ROW_TILES * ROWS], F32, name="result")
         for t in range(ROW_TILES):
             nc.vector.scalar_tensor_tensor(
-                out=with_cross[:, t * ROWS : (t + 1) * ROWS],
-                in0=cross[t][:],
-                scalar=2.0 * LAMDA,
-                in1=plain[:, t * ROWS : (t + 1) * ROWS],
-                op0=ALU.mult,
-                op1=ALU.add,
-            )
-        for t in range(ROW_TILES):
-            nc.vector.scalar_tensor_tensor(
                 out=result[:, t * ROWS : (t + 1) * ROWS],
-                in0=dot[t][:],
+                in0=product[t][:],
                 scalar=2.0,
-                in1=with_cross[:, t * ROWS : (t + 1) * ROWS],
+                in1=plain[:, t * ROWS : (t + 1) * ROWS],
                 op0=ALU.mult,
                 op1=ALU.add,
             )

@@ -36,6 +36,7 @@ FLOPS = 2 * 2 * ROWS * ROWS * D
 
 VARIANCES = ("xv", "pv")
 MEANS = ("x", "pm")
+SCALAR_TAKES_PM = 4
 VAR_BANKS = 3
 INPUTS = ("xv", "pv", "x", "pm")
 
@@ -157,14 +158,15 @@ def tile_probprotoseghead_k_kernel(tc, x, x_var, proto_mean, proto_var, out):
                     scale=LAMDA,
                 )
             mean_words = mean[:].bitcast(F32)
-            nc.scalar.copy(
-                out=mean_words[:, 0 : 2 * ROWS].rearrange("p (r u) -> p r u", u=2),
-                in_=in_psum[("x", g)][:].rearrange("p (u r) -> p r u", u=2),
-            )
-            nc.vector.tensor_copy(
-                out=mean_words[:, 2 * ROWS : 4 * ROWS].rearrange("p (r u) -> p r u", u=2),
-                in_=in_psum[("pm", g)][:].rearrange("p (u r) -> p r u", u=2),
-            )
+            for i, name in enumerate(MEANS):
+                on_scalar = name == "x" or g % SCALAR_TAKES_PM == SCALAR_TAKES_PM - 2
+                copy = nc.scalar.copy if on_scalar else nc.vector.tensor_copy
+                copy(
+                    out=mean_words[:, 2 * i * ROWS : 2 * (i + 1) * ROWS].rearrange(
+                        "p (r u) -> p r u", u=2
+                    ),
+                    in_=in_psum[(name, g)][:].rearrange("p (u r) -> p r u", u=2),
+                )
             grouped["mean"] = mean
             grouped["var"] = var
 

@@ -25,10 +25,8 @@ CHUNK = 1024
 CHUNK_WORDS = CHUNK // 2
 CHUNK_PASSES = CHUNK // K_PASS
 CHUNKS = D // CHUNK
-CHUNK_PAIRS = CHUNKS // 2
-SUM_LAG = 5
-TENSOR_PAIRS = 6
-FOLDED_PASSES = TENSOR_PAIRS * 2 * CHUNK_PASSES
+FOLDED_CHUNKS = 12
+FOLDED_PASSES = FOLDED_CHUNKS * CHUNK_PASSES
 CHUNK_BUFS = 8
 GROUPED = ROWS * 4
 
@@ -36,7 +34,6 @@ FLOPS = 2 * 2 * ROWS * ROWS * D
 
 VARIANCES = ("xv", "pv")
 MEANS = ("x", "pm")
-SCALAR_TAKES_PM = 4
 VAR_BANKS = 3
 INPUTS = ("xv", "pv", "x", "pm")
 
@@ -71,15 +68,9 @@ def tile_probprotoseghead_k_kernel(tc, x, x_var, proto_mean, proto_var, out):
 
         product = [sums.tile([P, ROWS], F32, name="product%d" % t) for t in range(ROW_TILES)]
 
-        pieces = const.tile([P, 2 * ROW_TILES * CHUNK_PAIRS], F32, name="pieces")
+        pieces = const.tile([P, 2 * ROW_TILES * CHUNKS], F32, name="pieces")
         nc.vector.memset(pieces[:], 0.0)
         folded = sums.tile([P, K_PASS], F32, name="folded")
-        vector_sums = [
-            (j, i)
-            for j in range(CHUNK_PAIRS)
-            for i in range(2 * ROW_TILES)
-            if i > 0 or j >= TENSOR_PAIRS
-        ]
 
         resident = {}
         in_psum = {}
@@ -95,22 +86,23 @@ def tile_probprotoseghead_k_kernel(tc, x, x_var, proto_mean, proto_var, out):
                 )
                 resident[(name, c)] = rows
 
-        def add_rows(k):
-            j, i = vector_sums[k]
-            name, t = VARIANCES[i // ROW_TILES], i % ROW_TILES
-            halves = [
-                resident[(name, c)][:, t * CHUNK : (t + 1) * CHUNK] for c in (2 * j, 2 * j + 1)
-            ]
-            pair_sums = stage.tile([P, CHUNK], F32, name="pair_sums")
-            nc.vector.scalar_tensor_tensor(
-                out=pair_sums[:],
-                in0=halves[0],
-                scalar=1.0,
-                in1=halves[1],
-                op0=ALU.mult,
-                op1=ALU.add,
-                accum_out=pieces[:, i * CHUNK_PAIRS + j : i * CHUNK_PAIRS + j + 1],
-            )
+        def add_rows(g):
+            c, v = divmod(g, CHUNK_PASSES)
+            rows = resident[(VARIANCES[v], c)]
+            for t in range(ROW_TILES):
+                i = v * ROW_TILES + t
+                if i == 0 and c < FOLDED_CHUNKS:
+                    continue
+                pair_sums = stage.tile([P, CHUNK // 2], F32, name="pair_sums")
+                nc.vector.scalar_tensor_tensor(
+                    out=pair_sums[:],
+                    in0=rows[:, t * CHUNK : t * CHUNK + CHUNK // 2],
+                    scalar=1.0,
+                    in1=rows[:, t * CHUNK + CHUNK // 2 : (t + 1) * CHUNK],
+                    op0=ALU.mult,
+                    op1=ALU.add,
+                    accum_out=pieces[:, i * CHUNKS + c : i * CHUNKS + c + 1],
+                )
 
         def fold_rows(g):
             c, local = divmod(g, CHUNK_PASSES)
@@ -145,6 +137,10 @@ def tile_probprotoseghead_k_kernel(tc, x, x_var, proto_mean, proto_var, out):
                         )
                 in_psum[(name, g)] = bank
 
+        def scalar_takes_pm(g):
+            c, v = divmod(g, CHUNK_PASSES)
+            return v == 1 and (c % 2 == 1 or c >= FOLDED_CHUNKS)
+
         def leave_psum(g):
             mean = stage.tile([P, 2 * GROUPED], BF16, name="mean", align_bytes=64)
             var = stage.tile([P, 2 * GROUPED], BF16, name="var", align_bytes=64)
@@ -159,7 +155,7 @@ def tile_probprotoseghead_k_kernel(tc, x, x_var, proto_mean, proto_var, out):
                 )
             mean_words = mean[:].bitcast(F32)
             for i, name in enumerate(MEANS):
-                on_scalar = name == "x" or g % SCALAR_TAKES_PM == SCALAR_TAKES_PM - 2
+                on_scalar = name == "x" or scalar_takes_pm(g)
                 copy = nc.scalar.copy if on_scalar else nc.vector.tensor_copy
                 copy(
                     out=mean_words[:, 2 * i * ROWS : 2 * (i + 1) * ROWS].rearrange(
@@ -200,7 +196,7 @@ def tile_probprotoseghead_k_kernel(tc, x, x_var, proto_mean, proto_var, out):
         def total_rows():
             nc.vector.tensor_reduce(
                 out=totals[:],
-                in_=pieces[:].rearrange("p (i j) -> p i j", j=CHUNK_PAIRS),
+                in_=pieces[:].rearrange("p (i c) -> p i c", c=CHUNKS),
                 axis=AXIS.X,
                 op=ALU.add,
             )
@@ -231,20 +227,16 @@ def tile_probprotoseghead_k_kernel(tc, x, x_var, proto_mean, proto_var, out):
                 transposes(g + 1, VARIANCES)
             if g >= 1:
                 quantise()
-            if 0 <= g - SUM_LAG < len(vector_sums):
-                add_rows(g - SUM_LAG)
-            if g == PASSES - SUM_LAG:
+            add_rows(g)
+            if g == FOLDED_PASSES + CHUNK_PASSES:
                 add_folded()
             leave_psum(g)
             if g >= 1:
                 multiply(g - 1)
             if g < FOLDED_PASSES:
                 fold_rows(g)
-            if 0 <= g - SUM_LAG < len(vector_sums):
-                j, i = vector_sums[g - SUM_LAG]
-                if i == 2 * ROW_TILES - 1 and 2 * j + CHUNK_BUFS < CHUNKS:
-                    load(2 * j + CHUNK_BUFS)
-                    load(2 * j + 1 + CHUNK_BUFS)
+            if (g + 1) % CHUNK_PASSES == 0 and g // CHUNK_PASSES + CHUNK_BUFS < CHUNKS:
+                load(g // CHUNK_PASSES + CHUNK_BUFS)
         total_rows()
 
         spread = banks.tile([P, ROWS], F32, name="spread", tag="x")

@@ -1,3 +1,4 @@
+import itertools
 from contextlib import ExitStack
 
 import concourse.mybir as mybir
@@ -88,11 +89,12 @@ def tile_probprotoseghead_k_kernel(tc, x, x_var, proto_mean, proto_var, out):
 
         def add_rows(g):
             c, v = divmod(g, CHUNK_PASSES)
-            rows = resident[(VARIANCES[v], c)]
-            for t in range(ROW_TILES):
+            kinds = ((0, 1), ()) if c == 0 else ((0,), (1,))
+            for v, t in itertools.product(kinds[v], range(ROW_TILES)):
                 i = v * ROW_TILES + t
                 if i == 0 and c < FOLDED_CHUNKS:
                     continue
+                rows = resident[(VARIANCES[v], c)]
                 pair_sums = stage.tile([P, CHUNK // 2], F32, name="pair_sums")
                 nc.vector.scalar_tensor_tensor(
                     out=pair_sums[:],
@@ -139,7 +141,7 @@ def tile_probprotoseghead_k_kernel(tc, x, x_var, proto_mean, proto_var, out):
 
         def scalar_takes_pm(g):
             c, v = divmod(g, CHUNK_PASSES)
-            return v == 1 and (c % 2 == 1 or c >= FOLDED_CHUNKS)
+            return v == 1 and c >= FOLDED_CHUNKS
 
         def leave_psum(g):
             mean = stage.tile([P, 2 * GROUPED], BF16, name="mean", align_bytes=64)

@@ -224,9 +224,14 @@ def tile_probprotoseghead_k_kernel(tc, x, x_var, proto_mean, proto_var, out):
 
         transposes(0, VARIANCES)
         for g in range(PASSES):
-            transposes(g, MEANS)
-            if g + 1 < PASSES:
-                transposes(g + 1, VARIANCES)
+            if g == 0:
+                transposes(1, VARIANCES[:1])
+                transposes(0, MEANS)
+                transposes(1, VARIANCES[1:])
+            else:
+                transposes(g, MEANS)
+                if g + 1 < PASSES:
+                    transposes(g + 1, VARIANCES)
             if g >= 1:
                 quantise()
             add_rows(g)
@@ -241,7 +246,7 @@ def tile_probprotoseghead_k_kernel(tc, x, x_var, proto_mean, proto_var, out):
                 load(g // CHUNK_PASSES + CHUNK_BUFS)
         total_rows()
 
-        spread = banks.tile([P, ROWS], F32, name="spread", tag="x")
+        spread = banks.tile([P, ROWS], F32, name="spread", tag="var", bufs=VAR_BANKS)
         for t in range(ROW_TILES):
             nc.tensor.transpose(
                 spread[:, t * P : (t + 1) * P], repeated[:, t * P : (t + 1) * P], identity[:]
@@ -251,12 +256,11 @@ def tile_probprotoseghead_k_kernel(tc, x, x_var, proto_mean, proto_var, out):
 
         plain = const.tile([P, ROW_TILES * ROWS], F32, name="plain")
         for t in range(ROW_TILES):
-            nc.vector.tensor_scalar(
+            nc.scalar.activation(
                 out=plain[:, t * ROWS : (t + 1) * ROWS],
-                in0=spread[:],
-                scalar1=row_term[:, t : t + 1],
-                scalar2=None,
-                op0=ALU.add,
+                in_=spread[:],
+                func=ACT.Identity,
+                bias=row_term[:, t : t + 1],
             )
         result = const.tile([P, ROW_TILES * ROWS], F32, name="result")
         for t in range(ROW_TILES):

@@ -141,7 +141,7 @@ def tile_probprotoseghead_k_kernel(tc, x, x_var, proto_mean, proto_var, out):
 
         def scalar_takes_pm(g):
             c, v = divmod(g, CHUNK_PASSES)
-            return v == 1 and c >= FOLDED_CHUNKS
+            return v == 1 and c >= FOLDED_CHUNKS - 1
 
         def leave_psum(g):
             mean = stage.tile([P, 2 * GROUPED], BF16, name="mean", align_bytes=64)

import itertools
from contextlib import ExitStack

import concourse.mybir as mybir
from concourse.masks import make_identity

F32 = mybir.dt.float32
BF16 = mybir.dt.bfloat16
U32 = mybir.dt.uint32
U8 = mybir.dt.uint8
FP8X4 = mybir.dt.float8_e4m3fn_x4
ACT = mybir.ActivationFunctionType
ALU = mybir.AluOpType
AXIS = mybir.AxisListType

LAMDA = 0.00390625

P = 128
ROWS = 256
ROW_TILES = ROWS // P
D = 16384
K_PASS = 4 * P
PASSES = D // K_PASS
PASS_WORDS = K_PASS // 2
CHUNK = 1024
CHUNK_WORDS = CHUNK // 2
CHUNK_PASSES = CHUNK // K_PASS
CHUNKS = D // CHUNK
FOLDED_CHUNKS = 12
FOLDED_PASSES = FOLDED_CHUNKS * CHUNK_PASSES
CHUNK_BUFS = 8
GROUPED = ROWS * 4

FLOPS = 2 * 2 * ROWS * ROWS * D

VARIANCES = ("xv", "pv")
MEANS = ("x", "pm")
VAR_BANKS = 3
INPUTS = ("xv", "pv", "x", "pm")


def tile_probprotoseghead_k_kernel(tc, x, x_var, proto_mean, proto_var, out):
    nc = tc.nc
    with ExitStack() as ctx:
        ctx.enter_context(tc.manual_schedule())
        const = ctx.enter_context(tc.tile_pool(name="const", bufs=1))
        chunks = ctx.enter_context(tc.tile_pool(name="chunks", bufs=CHUNK_BUFS))
        stage = ctx.enter_context(tc.tile_pool(name="stage", bufs=3))
        banks = ctx.enter_context(tc.psum_pool(name="banks", bufs=1))
        sums = ctx.enter_context(tc.psum_pool(name="sums", bufs=1))

        dram = {
            "x": x.rearrange("(t p) d -> p t d", p=P),
            "xv": x_var.rearrange("(t p) d -> p t d", p=P),
            "pm": proto_mean.rearrange("c m d -> (c m) d").rearrange("(t p) d -> p t d", p=P),
            "pv": proto_var.rearrange("c m d -> (c m) d").rearrange("(t p) d -> p t d", p=P),
        }
        out_rows = out.rearrange("(t p) c m -> p t (c m)", p=P)

        identity = const.tile([P, P], F32, name="identity")
        make_identity(nc, identity[:])
        identity_bf16 = const.tile([P, P], BF16, name="identity_bf16")
        make_identity(nc, identity_bf16[:])

        one = const.tile([P, 1], F32, name="one")
        nc.vector.memset(one[:], 1.0)
        warm = const.tile([P, 1], F32, name="warm")
        nc.scalar.activation(out=warm[:], in_=one[:], func=ACT.Sqrt)

        product = [sums.tile([P, ROWS], F32, name="product%d" % t) for t in range(ROW_TILES)]

        pieces = const.tile([P, 2 * ROW_TILES * CHUNKS], F32, name="pieces")
        nc.vector.memset(pieces[:], 0.0)
        folded = sums.tile([P, K_PASS], F32, name="folded")

        resident = {}
        in_psum = {}
        grouped = {}
        packed = {}

        def load(c):
            for name in INPUTS:
                rows = chunks.tile([P, ROW_TILES * CHUNK], BF16, name="rows_" + name, tag=name)
                nc.sync.dma_start(
                    out=rows[:].rearrange("p (t d) -> p t d", t=ROW_TILES),
                    in_=dram[name][:, :, c * CHUNK : (c + 1) * CHUNK],
                )
                resident[(name, c)] = rows

        def add_rows(g):
            c, v = divmod(g, CHUNK_PASSES)
            kinds = ((0, 1), ()) if c == 0 else ((0,), (1,))
            for v, t in itertools.product(kinds[v], range(ROW_TILES)):
                i = v * ROW_TILES + t
                if i == 0 and c < FOLDED_CHUNKS:
                    continue
                rows = resident[(VARIANCES[v], c)]
                pair_sums = stage.tile([P, CHUNK // 2], F32, name="pair_sums")
                nc.vector.scalar_tensor_tensor(
                    out=pair_sums[:],
                    in0=rows[:, t * CHUNK : t * CHUNK + CHUNK // 2],
                    scalar=1.0,
                    in1=rows[:, t * CHUNK + CHUNK // 2 : (t + 1) * CHUNK],
                    op0=ALU.mult,
                    op1=ALU.add,
                    accum_out=pieces[:, i * CHUNKS + c : i * CHUNKS + c + 1],
                )

        def fold_rows(g):
            c, local = divmod(g, CHUNK_PASSES)
            nc.tensor.matmul(
                folded[:],
                lhsT=identity_bf16[:],
                rhs=resident[("xv", c)][:, local * K_PASS : (local + 1) * K_PASS],
                start=(g == 0),
                stop=(g == FOLDED_PASSES - 1),
            )

        def add_folded():
            nc.vector.tensor_reduce(
                out=pieces[:, 0:1], in_=folded[:], axis=AXIS.X, op=ALU.add
            )

        def transposes(g, names):
            c, local = divmod(g, CHUNK_PASSES)
            for name in names:
                words = resident[(name, c)][:].bitcast(F32)
                if name in VARIANCES:
                    bank = banks.tile([P, 2 * ROWS], F32, name="bank_var", tag="var", bufs=VAR_BANKS)
                else:
                    bank = banks.tile([P, 2 * ROWS], F32, name="bank_" + name, tag=name)
                for u in range(2):
                    for t in range(ROW_TILES):
                        first = t * CHUNK_WORDS + local * PASS_WORDS + u * P
                        nc.tensor.transpose(
                            bank[:, u * ROWS + t * P : u * ROWS + (t + 1) * P],
                            words[:, first : first + P],
                            identity[:],
                        )
                in_psum[(name, g)] = bank

        def scalar_takes_pm(g):
            c, v = divmod(g, CHUNK_PASSES)
            return v == 1 and c >= FOLDED_CHUNKS - 1

        def leave_psum(g):
            mean = stage.tile([P, 2 * GROUPED], BF16, name="mean", align_bytes=64)
            var = stage.tile([P, 2 * GROUPED], BF16, name="var", align_bytes=64)
            for i, name in enumerate(VARIANCES):
                nc.scalar.activation(
                    out=var[:, i * GROUPED : (i + 1) * GROUPED].rearrange(
                        "p (r u e) -> p r u e", u=2, e=2
                    ),
                    in_=in_psum[(name, g)][:].bitcast(BF16).rearrange("p (u r e) -> p r u e", u=2, e=2),
                    func=ACT.Sqrt,
                    scale=LAMDA,
                )
            mean_words = mean[:].bitcast(F32)
            for i, name in enumerate(MEANS):
                on_scalar = name == "x" or scalar_takes_pm(g)
                copy = nc.scalar.copy if on_scalar else nc.vector.tensor_copy
                copy(
                    out=mean_words[:, 2 * i * ROWS : 2 * (i + 1) * ROWS].rearrange(
                        "p (r u) -> p r u", u=2
                    ),
                    in_=in_psum[(name, g)][:].rearrange("p (u r) -> p r u", u=2),
                )
            grouped["mean"] = mean
            grouped["var"] = var

        def quantise():
            for kind in ("var", "mean"):
                words = stage.tile([P, 2 * ROWS], U32, name="words_" + kind, align_bytes=64)
                scales = stage.tile([P, 2 * ROWS], U8, name="scales_" + kind, align_bytes=64)
                nc.vector.quantize_mx(
                    out=words[:].bitcast(FP8X4), scales=scales[:], in_=grouped[kind][:]
                )
                packed[kind] = (words, scales)

        def multiply(g):
            for kind in ("var", "mean"):
                words, scales = packed[kind]
                for t in range(ROW_TILES):
                    nc.tensor.matmul_mx(
                        out=product[t][:],
                        lhsT=words[:, t * P : (t + 1) * P].bitcast(FP8X4),
                        lhsT_scale=scales[:, t * P : (t + 1) * P],
                        rhs=words[:, ROWS : 2 * ROWS].bitcast(FP8X4),
                        rhs_scale=scales[:, ROWS : 2 * ROWS],
                        start=(g == 0 and kind == "var"),
                        stop=(g == PASSES - 1 and kind == "mean"),
                    )

        totals = const.tile([P, 2 * ROW_TILES], F32, name="totals")
        row_term = const.tile([P, ROW_TILES], F32, name="row_term")
        repeated = const.tile([P, ROWS], F32, name="repeated")

        def total_rows():
            nc.vector.tensor_reduce(
                out=totals[:],
                in_=pieces[:].rearrange("p (i c) -> p i c", c=CHUNKS),
                axis=AXIS.X,
                op=ALU.add,
            )
            nc.vector.tensor_scalar(
                out=row_term[:],
                in0=totals[:, 0:ROW_TILES],
                scalar1=-LAMDA,
                scalar2=-2.0,
                op0=ALU.mult,
                op1=ALU.add,
            )
            for t in range(ROW_TILES):
                nc.vector.tensor_scalar(
                    out=repeated[:, t * P : (t + 1) * P],
                    in0=totals[:, ROW_TILES + t : ROW_TILES + t + 1].to_broadcast([P, P]),
                    scalar1=-LAMDA,
                    scalar2=None,
                    op0=ALU.mult,
                )

        for c in range(CHUNK_BUFS):
            load(c)

        transposes(0, VARIANCES)
        for g in range(PASSES):
            if g == 0:
                transposes(1, VARIANCES[:1])
                transposes(0, MEANS)
                transposes(1, VARIANCES[1:])
            else:
                transposes(g, MEANS)
                if g + 1 < PASSES:
                    transposes(g + 1, VARIANCES)
            if g >= 1:
                quantise()
            add_rows(g)
            if g == FOLDED_PASSES + CHUNK_PASSES:
                add_folded()
            leave_psum(g)
            if g >= 1:
                multiply(g - 1)
            if g < FOLDED_PASSES:
                fold_rows(g)
            if (g + 1) % CHUNK_PASSES == 0 and g // CHUNK_PASSES + CHUNK_BUFS < CHUNKS:
                load(g // CHUNK_PASSES + CHUNK_BUFS)
        total_rows()

        spread = banks.tile([P, ROWS], F32, name="spread", tag="var", bufs=VAR_BANKS)
        for t in range(ROW_TILES):
            nc.tensor.transpose(
                spread[:, t * P : (t + 1) * P], repeated[:, t * P : (t + 1) * P], identity[:]
            )
        quantise()
        multiply(PASSES - 1)

        plain = const.tile([P, ROW_TILES * ROWS], F32, name="plain")
        for t in range(ROW_TILES):
            nc.scalar.activation(
                out=plain[:, t * ROWS : (t + 1) * ROWS],
                in_=spread[:],
                func=ACT.Identity,
                bias=row_term[:, t : t + 1],
            )
        result = const.tile([P, ROW_TILES * ROWS], F32, name="result")
        for t in range(ROW_TILES):
            nc.vector.scalar_tensor_tensor(
                out=result[:, t * ROWS : (t + 1) * ROWS],
                in0=product[t][:],
                scalar=2.0,
                in1=plain[:, t * ROWS : (t + 1) * ROWS],
                op0=ALU.mult,
                op1=ALU.add,
            )
            nc.sync.dma_start(out=out_rows[:, t, :], in_=result[:, t * ROWS : (t + 1) * ROWS])
